import numpy as np
import ml_dtypes

BF16 = ml_dtypes.bfloat16


def bf(x):
    return np.asarray(x, np.float32).astype(BF16)


def f32(x):
    return np.asarray(x, np.float32)


def f64(x):
    return np.asarray(x).astype(np.float64)


def striped(idx):
    return np.tile(idx.reshape(-1, 16).T, (8, 1))


D, S, N, M = 128, 256, 128, 384


def setup_inputs():
    return {"table": f32(np.random.standard_normal((D, S))), "values": f32(np.random.standard_normal((1, N))), "val_w": f32(np.random.standard_normal((D, 1))), "val_b": f32(0.1 * np.random.standard_normal((D, 1))), "w_qkv": bf(np.random.standard_normal((D, M)) / np.sqrt(D)), "b_qkv": f32(0.1 * np.random.standard_normal((M, 1))), "offs": striped(np.random.permutation(np.tile(np.arange(S), 2))[:N])}


def reference(table, values, val_w, val_b, w_qkv, b_qkv, offs):
    idx = offs[:16].T.reshape(-1)
    x = f64(table)[:, idx] + (f64(val_w) * f64(values) + f64(val_b))
    qkv = f64(w_qkv).T @ x + f64(b_qkv)
    return np.concatenate([x, qkv], axis=0)

@@ -1,0 +1,54 @@
+import concourse.mybir as mybir
+
+F32, BF16, U16 = mybir.dt.float32, mybir.dt.bfloat16, mybir.dt.uint16
+MULT, ADD = mybir.AluOpType.mult, mybir.AluOpType.add
+
+P = 128
+S = 256
+N = 128
+M = 384
+BLOCKS = M // P
+
+FLOPS = 2 * P * M * N
+
+
+def tile_tabulartransformerwithattention_kernel(tc, table, values, val_w, val_b, w_qkv, b_qkv, offs, out):
+    nc = tc.nc
+    with (
+        tc.tile_pool(name="held", bufs=1) as held,
+        tc.psum_pool(name="banks", bufs=BLOCKS) as banks,
+    ):
+        offsets = held.tile([P, N // 16], U16, name="offsets")
+        nc.sync.dma_start(offsets[:], offs)
+        window = held.tile([P, S], F32, name="window")
+        nc.sync.dma_start(window[:], table)
+
+        values_all = held.tile([P, N], F32, name="values_all")
+        nc.scalar.dma_start(values_all[:], values.rearrange("o n -> (o n)").partition_broadcast(P))
+        slope = held.tile([P, 1], F32, name="slope")
+        nc.scalar.dma_start(slope[:], val_w)
+        shift = held.tile([P, 1], F32, name="shift")
+        nc.scalar.dma_start(shift[:], val_b)
+
+        weights = held.tile([P, M], BF16, name="weights")
+        nc.gpsimd.dma_start(weights[:], w_qkv)
+        bias = held.tile([P, BLOCKS], F32, name="bias")
+        with nc.allow_non_contiguous_dma(reason="384 biases, one to a partition and block"):
+            nc.gpsimd.dma_start(bias[:], b_qkv.rearrange("(b p) o -> p (b o)", p=P))
+
+        term = held.tile([P, N], F32, name="term")
+        nc.vector.tensor_scalar(term[:], values_all[:], slope[:], shift[:], MULT, ADD)
+
+        x = held.tile([P, N], F32, name="x")
+        nc.vector.tensor_tensor(x[:], window[:].indirect(offsets[:]), term[:], ADD)
+        nc.sync.dma_start(out[0:P, :], x[:])
+
+        x_bf = held.tile([P, N], BF16, name="x_bf")
+        nc.vector.tensor_copy(x_bf[:], x[:])
+
+        qkv = held.tile([P, BLOCKS, N], F32, name="qkv")
+        for b in range(BLOCKS):
+            bank = banks.tile([P, N], F32, name="bank")
+            nc.tensor.matmul(bank[:], weights[:, b * P : (b + 1) * P], x_bf[:], start=True, stop=True)
+            nc.vector.tensor_scalar(qkv[:, b, :], bank[:], bias[:, b : b + 1], None, ADD)
+        nc.sync.dma_start(out[P : P + M, :].rearrange("(b p) j -> p b j", p=P), qkv[:])

@@ -33,8 +33,7 @@ def tile_tabulartransformerwithattention_kernel(tc, table, values, val_w, val_b,
         weights = held.tile([P, M], BF16, name="weights")
         nc.gpsimd.dma_start(weights[:], w_qkv)
         bias = held.tile([P, BLOCKS], F32, name="bias")
-        with nc.allow_non_contiguous_dma(reason="384 biases, one to a partition and block"):
-            nc.gpsimd.dma_start(bias[:], b_qkv.rearrange("(b p) o -> p (b o)", p=P))
+        nc.gpsimd.dma_start(bias[:], b_qkv.rearrange("(p b) o -> p (b o)", b=BLOCKS))
 
         term = held.tile([P, N], F32, name="term")
         nc.vector.tensor_scalar(term[:], values_all[:], slope[:], shift[:], MULT, ADD)
@@ -49,6 +48,6 @@ def tile_tabulartransformerwithattention_kernel(tc, table, values, val_w, val_b,
         qkv = held.tile([P, BLOCKS, N], F32, name="qkv")
         for b in range(BLOCKS):
             bank = banks.tile([P, N], F32, name="bank")
-            nc.tensor.matmul(bank[:], weights[:, b * P : (b + 1) * P], x_bf[:], start=True, stop=True)
+            nc.tensor.matmul(bank[:], weights[:, b:M:BLOCKS], x_bf[:], start=True, stop=True)
             nc.vector.tensor_scalar(qkv[:, b, :], bank[:], bias[:, b : b + 1], None, ADD)
-        nc.sync.dma_start(out[P : P + M, :].rearrange("(b p) j -> p b j", p=P), qkv[:])
+        nc.sync.dma_start(out[P : P + M, :].rearrange("(p b) j -> p b j", b=BLOCKS), qkv[:])

@@ -7,6 +7,7 @@ P = 128
 S = 256
 N = 128
 M = 384
+SQUARE = 32
 BLOCKS = M // P
 
 FLOPS = 2 * P * M * N
@@ -25,18 +26,22 @@ def tile_tabulartransformerwithattention_kernel(tc, table, values, val_w, val_b,
 
         values_all = held.tile([P, N], F32, name="values_all")
         nc.scalar.dma_start(values_all[:], values.rearrange("o n -> (o n)").partition_broadcast(P))
-        slope = held.tile([P, 1], F32, name="slope")
-        nc.scalar.dma_start(slope[:], val_w)
-        shift = held.tile([P, 1], F32, name="shift")
-        nc.scalar.dma_start(shift[:], val_b)
+
+        lying = held.tile([P, SQUARE], F32, name="lying", align_bytes=64)
+        nc.vector.memset(lying[:], 0.0)
+        nc.scalar.dma_start(lying[0:P:SQUARE, :], val_w.rearrange("(q i) o -> q (i o)", i=SQUARE))
+        nc.scalar.dma_start(lying[1:P:SQUARE, :], val_b.rearrange("(q i) o -> q (i o)", i=SQUARE))
 
         weights = held.tile([P, M], BF16, name="weights")
         nc.gpsimd.dma_start(weights[:], w_qkv)
         bias = held.tile([P, BLOCKS], F32, name="bias")
         nc.gpsimd.dma_start(bias[:], b_qkv.rearrange("(p b) o -> p (b o)", b=BLOCKS))
 
+        standing = held.tile([P, SQUARE], F32, name="standing", align_bytes=64)
+        nc.vector.transpose(standing[:], lying[:])
+        slope, shift = standing[:, 0:1], standing[:, 1:2]
         term = held.tile([P, N], F32, name="term")
-        nc.vector.tensor_scalar(term[:], values_all[:], slope[:], shift[:], MULT, ADD)
+        nc.vector.tensor_scalar(term[:], values_all[:], slope, shift, MULT, ADD)
 
         x = held.tile([P, N], F32, name="x")
         nc.vector.tensor_tensor(x[:], window[:].indirect(offsets[:]), term[:], ADD)

@@ -24,22 +24,25 @@ def tile_tabulartransformerwithattention_kernel(tc, table, values, val_w, val_b,
         window = held.tile([P, S], F32, name="window")
         nc.sync.dma_start(window[:], table)
 
-        values_all = held.tile([P, N], F32, name="values_all")
-        nc.scalar.dma_start(values_all[:], values.rearrange("o n -> (o n)").partition_broadcast(P))
-
-        lying = held.tile([P, SQUARE], F32, name="lying", align_bytes=64)
+        lying = held.tile([P, N], F32, name="lying", align_bytes=64)
         nc.vector.memset(lying[:], 0.0)
-        nc.scalar.dma_start(lying[0:P:SQUARE, :], val_w.rearrange("(q i) o -> q (i o)", i=SQUARE))
-        nc.scalar.dma_start(lying[1:P:SQUARE, :], val_b.rearrange("(q i) o -> q (i o)", i=SQUARE))
+        nc.scalar.dma_start(lying[0:P:SQUARE, :], values.rearrange("o n -> (o n)").partition_broadcast(P // SQUARE))
+        nc.scalar.dma_start(lying[1:P:SQUARE, 0:SQUARE], val_w.rearrange("(q i) o -> q (i o)", i=SQUARE))
+        nc.scalar.dma_start(lying[2:P:SQUARE, 0:SQUARE], val_b.rearrange("(q i) o -> q (i o)", i=SQUARE))
 
         weights = held.tile([P, M], BF16, name="weights")
         nc.gpsimd.dma_start(weights[:], w_qkv)
         bias = held.tile([P, BLOCKS], F32, name="bias")
         nc.gpsimd.dma_start(bias[:], b_qkv.rearrange("(p b) o -> p (b o)", b=BLOCKS))
 
-        standing = held.tile([P, SQUARE], F32, name="standing", align_bytes=64)
+        standing = held.tile([P, N], F32, name="standing", align_bytes=64)
         nc.vector.transpose(standing[:], lying[:])
-        slope, shift = standing[:, 0:1], standing[:, 1:2]
+        slope, shift = standing[:, 1:2], standing[:, 2:3]
+        repeated = held.tile([P, N // SQUARE, SQUARE], F32, name="repeated", align_bytes=64)
+        first_columns = standing[:].rearrange("p (s r) -> p s r", r=SQUARE)[:, :, 0:1]
+        nc.vector.tensor_copy(repeated[:], first_columns.to_broadcast([P, N // SQUARE, SQUARE]))
+        values_all = held.tile([P, N], F32, name="values_all", align_bytes=64)
+        nc.vector.transpose(values_all[:], repeated[:].rearrange("p s i -> p (s i)"))
         term = held.tile([P, N], F32, name="term")
         nc.vector.tensor_scalar(term[:], values_all[:], slope, shift, MULT, ADD)
 

@@ -7,7 +7,7 @@ P = 128
 S = 256
 N = 128
 M = 384
-SQUARE = 32
+ROWS = 32
 BLOCKS = M // P
 
 FLOPS = 2 * P * M * N
@@ -24,27 +24,23 @@ def tile_tabulartransformerwithattention_kernel(tc, table, values, val_w, val_b,
         window = held.tile([P, S], F32, name="window")
         nc.sync.dma_start(window[:], table)
 
-        lying = held.tile([P, N], F32, name="lying", align_bytes=64)
-        nc.vector.memset(lying[:], 0.0)
-        nc.scalar.dma_start(lying[0:P:SQUARE, :], values.rearrange("o n -> (o n)").partition_broadcast(P // SQUARE))
-        nc.scalar.dma_start(lying[1:P:SQUARE, 0:SQUARE], val_w.rearrange("(q i) o -> q (i o)", i=SQUARE))
-        nc.scalar.dma_start(lying[2:P:SQUARE, 0:SQUARE], val_b.rearrange("(q i) o -> q (i o)", i=SQUARE))
+        factors = held.tile([ROWS, P], F32, name="factors")
+        nc.scalar.dma_start(factors[ROWS - 1 : ROWS, :], val_w.rearrange("c o -> o c"))
+        nc.scalar.dma_start(factors[ROWS - 2 : ROWS - 1, :], val_b.rearrange("c o -> o c"))
+        nc.vector.memset(factors[0 : ROWS - 2, :], 0.0)
+        tokens = held.tile([ROWS, N], F32, name="tokens")
+        nc.scalar.dma_start(tokens[ROWS - 1 : ROWS, :], values)
+        nc.vector.memset(tokens[0 : ROWS - 1, :], 1.0)
 
         weights = held.tile([P, M], BF16, name="weights")
         nc.gpsimd.dma_start(weights[:], w_qkv)
         bias = held.tile([P, BLOCKS], F32, name="bias")
         nc.gpsimd.dma_start(bias[:], b_qkv.rearrange("(p b) o -> p (b o)", b=BLOCKS))
 
-        standing = held.tile([P, N], F32, name="standing", align_bytes=64)
-        nc.vector.transpose(standing[:], lying[:])
-        slope, shift = standing[:, 1:2], standing[:, 2:3]
-        repeated = held.tile([P, N // SQUARE, SQUARE], F32, name="repeated", align_bytes=64)
-        first_columns = standing[:].rearrange("p (s r) -> p s r", r=SQUARE)[:, :, 0:1]
-        nc.vector.tensor_copy(repeated[:], first_columns.to_broadcast([P, N // SQUARE, SQUARE]))
-        values_all = held.tile([P, N], F32, name="values_all", align_bytes=64)
-        nc.vector.transpose(values_all[:], repeated[:].rearrange("p s i -> p (s i)"))
+        term_bank = banks.tile([P, N], F32, name="term_bank")
+        nc.tensor.matmul(term_bank[:], factors[:], tokens[:], start=True, stop=True)
         term = held.tile([P, N], F32, name="term")
-        nc.vector.tensor_scalar(term[:], values_all[:], slope, shift, MULT, ADD)
+        nc.vector.tensor_copy(term[:], term_bank[:])
 
         x = held.tile([P, N], F32, name="x")
         nc.vector.tensor_tensor(x[:], window[:].indirect(offsets[:]), term[:], ADD)

@@ -19,18 +19,18 @@ def tile_tabulartransformerwithattention_kernel(tc, table, values, val_w, val_b,
         tc.tile_pool(name="held", bufs=1) as held,
         tc.psum_pool(name="banks", bufs=BLOCKS) as banks,
     ):
-        offsets = held.tile([P, N // 16], U16, name="offsets")
-        nc.sync.dma_start(offsets[:], offs)
-        window = held.tile([P, S], F32, name="window")
-        nc.sync.dma_start(window[:], table)
-
         factors = held.tile([ROWS, P], F32, name="factors")
         nc.scalar.dma_start(factors[ROWS - 1 : ROWS, :], val_w.rearrange("c o -> o c"))
-        nc.scalar.dma_start(factors[ROWS - 2 : ROWS - 1, :], val_b.rearrange("c o -> o c"))
+        nc.sync.dma_start(factors[ROWS - 2 : ROWS - 1, :], val_b.rearrange("c o -> o c"))
         nc.vector.memset(factors[0 : ROWS - 2, :], 0.0)
         tokens = held.tile([ROWS, N], F32, name="tokens")
         nc.scalar.dma_start(tokens[ROWS - 1 : ROWS, :], values)
         nc.vector.memset(tokens[0 : ROWS - 1, :], 1.0)
+
+        offsets = held.tile([P, N // 16], U16, name="offsets")
+        nc.sync.dma_start(offsets[:], offs)
+        window = held.tile([P, S], F32, name="window")
+        nc.sync.dma_start(window[:], table)
 
         weights = held.tile([P, M], BF16, name="weights")
         nc.gpsimd.dma_start(weights[:], w_qkv)

@@ -20,7 +20,7 @@ def tile_tabulartransformerwithattention_kernel(tc, table, values, val_w, val_b,
         tc.psum_pool(name="banks", bufs=BLOCKS) as banks,
     ):
         factors = held.tile([ROWS, P], F32, name="factors")
-        nc.scalar.dma_start(factors[ROWS - 1 : ROWS, :], val_w.rearrange("c o -> o c"))
+        nc.sync.dma_start(factors[ROWS - 1 : ROWS, :], val_w.rearrange("c o -> o c"))
         nc.sync.dma_start(factors[ROWS - 2 : ROWS - 1, :], val_b.rearrange("c o -> o c"))
         nc.vector.memset(factors[0 : ROWS - 2, :], 0.0)
         tokens = held.tile([ROWS, N], F32, name="tokens")

@@ -8,6 +8,7 @@ S = 256
 N = 128
 M = 384
 ROWS = 32
+HALF = N // 2
 BLOCKS = M // P
 
 FLOPS = 2 * P * M * N
@@ -17,7 +18,7 @@ def tile_tabulartransformerwithattention_kernel(tc, table, values, val_w, val_b,
     nc = tc.nc
     with (
         tc.tile_pool(name="held", bufs=1) as held,
-        tc.psum_pool(name="banks", bufs=BLOCKS) as banks,
+        tc.psum_pool(name="banks", bufs=1) as banks,
     ):
         factors = held.tile([ROWS, P], F32, name="factors")
         nc.sync.dma_start(factors[ROWS - 1 : ROWS, :], val_w.rearrange("c o -> o c"))
@@ -37,21 +38,32 @@ def tile_tabulartransformerwithattention_kernel(tc, table, values, val_w, val_b,
         bias = held.tile([P, BLOCKS], F32, name="bias")
         nc.gpsimd.dma_start(bias[:], b_qkv.rearrange("(p b) o -> p (b o)", b=BLOCKS))
 
+        term = held.tile([P, N], F32, name="term")
+        x = held.tile([P, N], F32, name="x")
+        x_bf = held.tile([P, N], BF16, name="x_bf")
+
         term_bank = banks.tile([P, N], F32, name="term_bank")
         nc.tensor.matmul(term_bank[:], factors[:], tokens[:], start=True, stop=True)
-        term = held.tile([P, N], F32, name="term")
         nc.vector.tensor_copy(term[:], term_bank[:])
 
-        x = held.tile([P, N], F32, name="x")
-        nc.vector.tensor_tensor(x[:], window[:].indirect(offsets[:]), term[:], ADD)
+        def look_up(h):
+            picked = window[:].indirect(offsets[:, h * HALF // 16 : (h + 1) * HALF // 16])
+            nc.vector.tensor_tensor(x[:, h * HALF : (h + 1) * HALF], picked, term[:, h * HALF : (h + 1) * HALF], ADD)
+
+        def round_x(h):
+            nc.vector.tensor_copy(x_bf[:, h * HALF : (h + 1) * HALF], x[:, h * HALF : (h + 1) * HALF])
+
+        look_up(0)
+        look_up(1)
+        round_x(0)
+        round_x(1)
         nc.sync.dma_start(out[0:P, :], x[:])
 
-        x_bf = held.tile([P, N], BF16, name="x_bf")
-        nc.vector.tensor_copy(x_bf[:], x[:])
-
         qkv = held.tile([P, BLOCKS, N], F32, name="qkv")
-        for b in range(BLOCKS):
-            bank = banks.tile([P, N], F32, name="bank")
-            nc.tensor.matmul(bank[:], weights[:, b:M:BLOCKS], x_bf[:], start=True, stop=True)
-            nc.vector.tensor_scalar(qkv[:, b, :], bank[:], bias[:, b : b + 1], None, ADD)
+        for h in range(2):
+            half = slice(h * HALF, (h + 1) * HALF)
+            for b in range(BLOCKS):
+                bank = banks.tile([P, HALF], F32, name=f"bank{h}{b}")
+                nc.tensor.matmul(bank[:], weights[:, b:M:BLOCKS], x_bf[:, half], start=True, stop=True)
+                nc.vector.tensor_scalar(qkv[:, b, half], bank[:], bias[:, b : b + 1], None, ADD)
         nc.sync.dma_start(out[P : P + M, :].rearrange("(p b) j -> p b j", b=BLOCKS), qkv[:])

@@ -36,7 +36,7 @@ def tile_tabulartransformerwithattention_kernel(tc, table, values, val_w, val_b,
         weights = held.tile([P, M], BF16, name="weights")
         nc.gpsimd.dma_start(weights[:], w_qkv)
         bias = held.tile([P, BLOCKS], F32, name="bias")
-        nc.gpsimd.dma_start(bias[:], b_qkv.rearrange("(p b) o -> p (b o)", b=BLOCKS))
+        nc.scalar.dma_start(bias[:], b_qkv.rearrange("(p b) o -> p (b o)", b=BLOCKS))
 
         term = held.tile([P, N], F32, name="term")
         x = held.tile([P, N], F32, name="x")

import concourse.mybir as mybir

F32, BF16, U16 = mybir.dt.float32, mybir.dt.bfloat16, mybir.dt.uint16
MULT, ADD = mybir.AluOpType.mult, mybir.AluOpType.add

P = 128
S = 256
N = 128
M = 384
ROWS = 32
HALF = N // 2
BLOCKS = M // P

FLOPS = 2 * P * M * N


def tile_tabulartransformerwithattention_kernel(tc, table, values, val_w, val_b, w_qkv, b_qkv, offs, out):
    nc = tc.nc
    with (
        tc.tile_pool(name="held", bufs=1) as held,
        tc.psum_pool(name="banks", bufs=1) as banks,
    ):
        factors = held.tile([ROWS, P], F32, name="factors")
        nc.sync.dma_start(factors[ROWS - 1 : ROWS, :], val_w.rearrange("c o -> o c"))
        nc.sync.dma_start(factors[ROWS - 2 : ROWS - 1, :], val_b.rearrange("c o -> o c"))
        nc.vector.memset(factors[0 : ROWS - 2, :], 0.0)
        tokens = held.tile([ROWS, N], F32, name="tokens")
        nc.scalar.dma_start(tokens[ROWS - 1 : ROWS, :], values)
        nc.vector.memset(tokens[0 : ROWS - 1, :], 1.0)

        offsets = held.tile([P, N // 16], U16, name="offsets")
        nc.sync.dma_start(offsets[:], offs)
        window = held.tile([P, S], F32, name="window")
        nc.sync.dma_start(window[:], table)

        weights = held.tile([P, M], BF16, name="weights")
        nc.gpsimd.dma_start(weights[:], w_qkv)
        bias = held.tile([P, BLOCKS], F32, name="bias")
        nc.scalar.dma_start(bias[:], b_qkv.rearrange("(p b) o -> p (b o)", b=BLOCKS))

        term = held.tile([P, N], F32, name="term")
        x = held.tile([P, N], F32, name="x")
        x_bf = held.tile([P, N], BF16, name="x_bf")

        term_bank = banks.tile([P, N], F32, name="term_bank")
        nc.tensor.matmul(term_bank[:], factors[:], tokens[:], start=True, stop=True)
        nc.vector.tensor_copy(term[:], term_bank[:])

        def look_up(h):
            picked = window[:].indirect(offsets[:, h * HALF // 16 : (h + 1) * HALF // 16])
            nc.vector.tensor_tensor(x[:, h * HALF : (h + 1) * HALF], picked, term[:, h * HALF : (h + 1) * HALF], ADD)

        def round_x(h):
            nc.vector.tensor_copy(x_bf[:, h * HALF : (h + 1) * HALF], x[:, h * HALF : (h + 1) * HALF])

        look_up(0)
        look_up(1)
        round_x(0)
        round_x(1)
        nc.sync.dma_start(out[0:P, :], x[:])

        qkv = held.tile([P, BLOCKS, N], F32, name="qkv")
        for h in range(2):
            half = slice(h * HALF, (h + 1) * HALF)
            for b in range(BLOCKS):
                bank = banks.tile([P, HALF], F32, name=f"bank{h}{b}")
                nc.tensor.matmul(bank[:], weights[:, b:M:BLOCKS], x_bf[:, half], start=True, stop=True)
                nc.vector.tensor_scalar(qkv[:, b, half], bank[:], bias[:, b : b + 1], None, ADD)
        nc.sync.dma_start(out[P : P + M, :].rearrange("(p b) j -> p b j", b=BLOCKS), qkv[:])
